import numpy as np
import ml_dtypes


def mxq(x, axis, fmt="e4m3"):
    dtype, down = {"e4m3": (ml_dtypes.float8_e4m3fn, 7), "e5m2": (ml_dtypes.float8_e5m2, 14)}[fmt]
    v = np.moveaxis(np.asarray(x, np.float32).astype(ml_dtypes.bfloat16).astype(np.float64), axis, -1)
    blocks = v.reshape(v.shape[:-1] + (-1, 32))
    amax = np.abs(blocks).max(-1, keepdims=True)
    byte = np.maximum(np.where(amax > 0, np.frexp(amax)[1] - 1 + 127, 0) - down, 1)
    scale = np.exp2(byte - 127.0)
    codes = (blocks / scale).astype(np.float32).astype(dtype).astype(np.float64)
    return np.moveaxis((codes * scale).reshape(v.shape), -1, axis)


WIDE = False


def mx_kscale(k):
    if not WIDE:
        return np.ones(k)
    levels = np.array([10, -10, 5, -5, 0])
    a = np.random.permutation(np.resize(levels, k // 512 * 4)).reshape(k // 512, 4)
    idx = np.arange(k)
    return np.exp2(a[idx // 512, idx % 128 // 32])


BF16 = ml_dtypes.bfloat16


def bf(x):
    return np.asarray(x, np.float32).astype(BF16)


def f64(x):
    return np.asarray(x).astype(np.float64)


E2M1 = np.array([0.0, 0.5, 1.0, 1.5, 2.0, 3.0, 4.0, 6.0, -0.0, -0.5, -1.0, -1.5, -2.0, -3.0, -4.0, -6.0])


def pack_weight(w, fmt):
    k, n = w.shape
    w = f64(bf(w)).reshape(k // 32, 32, n)
    amax = np.abs(w).max(1)
    if fmt == "e4m3":
        byte = np.frexp(amax)[1] - 1 + 127 - 7
    else:
        mant, ex = np.frexp(amax / 6.0)
        byte = np.where(mant > 0.5, ex, ex - 1) + 127
    byte = np.clip(np.where(amax > 0, byte, 1), 1, 254)
    scaled = (w * np.exp2(127.0 - byte)[:, None, :]).reshape(k, n).astype(np.float32)
    by_word = np.ascontiguousarray(scaled.reshape(k // 512, 128, 4, n).transpose(0, 1, 3, 2))
    if fmt == "e4m3":
        words = by_word.astype(ml_dtypes.float8_e4m3fn).view(np.uint8)
    else:
        c = by_word.astype(ml_dtypes.float4_e2m1fn).view(np.uint8) & 0xF
        words = c[..., 0::2] | (c[..., 1::2] << 4)
    return np.ascontiguousarray(words), np.ascontiguousarray(byte.astype(np.uint8).reshape(k // 512, 16, n))


def unpack_weight(words, scales, fmt):
    g, p, n, _ = words.shape
    if fmt == "e4m3":
        vals = np.ascontiguousarray(words).view(ml_dtypes.float8_e4m3fn).astype(np.float64)
    else:
        nib = np.empty((g, p, n, 4), np.uint8)
        nib[..., 0::2] = words & 0xF
        nib[..., 1::2] = words >> 4
        vals = E2M1[nib]
    vals = vals * np.repeat(np.exp2(scales.astype(np.float64) - 127.0), 8, axis=1)[..., None]
    return vals.transpose(0, 1, 3, 2).reshape(g * 512, n)


B, C, D, T, H, W, P = 1, 16384, 128, 8, 8, 8, 2
N = T * H * W
NP = T * (H // P) * (W // P)
FMT = "e4m3"


def conv1x1(wq, b, xq):
    return ((wq @ xq) + b[None, :, None]).reshape(B, D, T, H, W)


def maxpool(v):
    return v.reshape(B, D, T, H // P, P, W // P, P).max(axis=(4, 6))


def setup_inputs():
    s = mx_kscale(C)
    a = 1.0 / np.sqrt(C) / s[None, :]
    x = bf(np.random.standard_normal((B, C, T, H, W)) * s[None, :, None, None, None])
    g_w_words, g_w_scales = pack_weight(np.ascontiguousarray((np.random.standard_normal((D, C)) * 0.15 * a).T), FMT)
    g_b = bf(np.random.standard_normal(D) * 0.03)
    theta_w_words, theta_w_scales = pack_weight(np.ascontiguousarray((np.random.standard_normal((D, C)) * 2.0 * a).T), FMT)
    theta_b = bf(np.random.standard_normal(D) * 0.2)
    phi_w_words, phi_w_scales = pack_weight(np.ascontiguousarray((np.random.standard_normal((D, C)) * a).T), FMT)
    phi_b = bf(np.random.standard_normal(D) * 0.1)
    return {"x": x,
            "g_w_words": g_w_words,
            "g_w_scales": g_w_scales,
            "g_b": g_b,
            "theta_w_words": theta_w_words,
            "theta_w_scales": theta_w_scales,
            "theta_b": theta_b,
            "phi_w_words": phi_w_words,
            "phi_w_scales": phi_w_scales,
            "phi_b": phi_b}


def reference(x, g_w_words, g_w_scales, g_b, theta_w_words, theta_w_scales, theta_b, phi_w_words, phi_w_scales, phi_b):
    xq = mxq(f64(x).reshape(B, C, N), 1, "e4m3")
    g_x = maxpool(conv1x1(unpack_weight(g_w_words, g_w_scales, FMT).T, f64(g_b), xq)).reshape(B, D, NP)
    theta_x = conv1x1(unpack_weight(theta_w_words, theta_w_scales, FMT).T, f64(theta_b), xq).reshape(B, D, N)
    phi_x = maxpool(conv1x1(unpack_weight(phi_w_words, phi_w_scales, FMT).T, f64(phi_b), xq)).reshape(B, D, NP)
    return g_x, theta_x, phi_x

@@ -1,0 +1,181 @@
+from contextlib import ExitStack
+
+import concourse.mybir as mybir
+
+BF16 = mybir.dt.bfloat16
+F32 = mybir.dt.float32
+I32 = mybir.dt.int32
+U32 = mybir.dt.uint32
+U8 = mybir.dt.uint8
+FP8X4 = mybir.dt.float8_e4m3fn_x4
+
+P = 128
+PACK = 4
+CHANNELS = 16384
+PASSES = CHANNELS // (P * PACK)
+POSITIONS = 8 * 8 * 8
+OUT_CHANNELS = 128
+CHUNK = 4
+CHUNKS = PASSES // CHUNK
+LEAD = 2
+QUANTISE_LAG = 2
+RAW_CHUNKS = 6
+QUANTISED_PASSES = 16
+
+FLOPS = 2 * 3 * OUT_CHANNELS * CHANNELS * POSITIONS
+
+
+def tile_nonlocalblocknd_pa_k_kernel(
+    tc,
+    x,
+    g_w_words,
+    g_w_scales,
+    g_b,
+    theta_w_words,
+    theta_w_scales,
+    theta_b,
+    phi_w_words,
+    phi_w_scales,
+    phi_b,
+    out_0,
+    out_1,
+    out_2,
+):
+    nc = tc.nc
+
+    convs = (
+        ("g", g_w_words, g_w_scales, g_b, out_0, True),
+        ("phi", phi_w_words, phi_w_scales, phi_b, out_2, True),
+        ("theta", theta_w_words, theta_w_scales, theta_b, out_1, False),
+    )
+
+    x_by_pass = x.rearrange("b c f h w -> (b c) (f h w)").rearrange(
+        "(i p t) n -> p i (t n)", p=P, t=PACK
+    )
+
+    with ExitStack() as ctx:
+        keep = ctx.enter_context(tc.tile_pool(name="keep", bufs=1))
+        raw_pool = ctx.enter_context(tc.tile_pool(name="raw", bufs=RAW_CHUNKS))
+        words_pool = ctx.enter_context(tc.tile_pool(name="words", bufs=CHUNKS))
+        grouped_pool = ctx.enter_context(tc.tile_pool(name="grouped", bufs=QUANTISE_LAG + 2))
+        quantised_pool = ctx.enter_context(tc.tile_pool(name="quantised", bufs=QUANTISED_PASSES))
+        result_pool = ctx.enter_context(tc.tile_pool(name="result", bufs=2))
+        psum = ctx.enter_context(tc.psum_pool(name="psum", bufs=1))
+        ctx.enter_context(tc.manual_schedule())
+
+        bias_bf16 = keep.tile([P, len(convs), 16], BF16)
+        for j, (name, words, scales, bias, out, pooled) in enumerate(convs):
+            nc.scalar.dma_start(out=bias_bf16[:, j, 0:1], in_=bias.rearrange("(p o) -> p o", o=1))
+        bias_f32 = keep.tile([P, len(convs)], F32)
+        nc.scalar.activation(
+            out=bias_f32[:],
+            in_=bias_bf16[:, :, 0],
+            func=mybir.ActivationFunctionType.Identity,
+        )
+
+        w_scales = {}
+        for name, words, scales, bias, out, pooled in convs:
+            w_scales[name] = keep.tile(
+                [P, PASSES, OUT_CHANNELS], U8, name="w_scales_" + name, align_bytes=64
+            )
+            nc.vector.memset(w_scales[name][:].bitcast(I32), 0)
+        for name, words, scales, bias, out, pooled in convs:
+            for quadrant in range(4):
+                nc.gpsimd.dma_start(
+                    out=w_scales[name][32 * quadrant : 32 * quadrant + 4].bitcast(F32),
+                    in_=scales.bitcast(F32)[:, 4 * quadrant : 4 * quadrant + 4, :].rearrange(
+                        "i r n -> r i n"
+                    ),
+                )
+
+        acc = {}
+        for name, words, scales, bias, out, pooled in convs:
+            acc[name] = psum.tile([P, POSITIONS], F32, name="acc_" + name)
+
+        raw = {}
+        w_words = {}
+        grouped = {}
+        x_words = {}
+        x_scales = {}
+
+        def load_x(chunk):
+            passes = slice(chunk * CHUNK, (chunk + 1) * CHUNK)
+            raw[chunk] = raw_pool.tile([P, CHUNK, PACK * POSITIONS], BF16, name="raw")
+            nc.sync.dma_start(out=raw[chunk][:], in_=x_by_pass[:, passes, :])
+
+        def load_weights(chunk):
+            passes = slice(chunk * CHUNK, (chunk + 1) * CHUNK)
+            for name, words, scales, bias, out, pooled in convs:
+                w_words[name, chunk] = words_pool.tile(
+                    [P, CHUNK, OUT_CHANNELS], U32, name="w_words_" + name, align_bytes=64
+                )
+                nc.sync.dma_start(
+                    out=w_words[name, chunk][:].bitcast(I32),
+                    in_=words.rearrange("i p n t -> i p (n t)")
+                    .bitcast(I32)
+                    .rearrange("i p n -> p i n")[:, passes, :],
+                )
+
+        def regroup(i):
+            grouped[i] = grouped_pool.tile([P, POSITIONS * PACK], BF16, name="grouped", align_bytes=64)
+            source = raw[i // CHUNK][:, i % CHUNK, :].rearrange("p (t c r) -> p c t r", t=PACK, r=4)
+            target = grouped[i][:].rearrange("p (c r t) -> p c t r", t=PACK, r=4)
+            if i % 2 == 0:
+                nc.vector.tensor_copy(out=target, in_=source)
+            else:
+                nc.scalar.copy(out=target, in_=source)
+
+        def quantise(i):
+            x_words[i] = quantised_pool.tile([P, POSITIONS], U32, name="x_words", align_bytes=64)
+            x_scales[i] = quantised_pool.tile([P, POSITIONS], U8, name="x_scales", align_bytes=64)
+            nc.vector.quantize_mx(
+                out=x_words[i][:].bitcast(FP8X4), scales=x_scales[i][:], in_=grouped[i][:]
+            )
+
+        def multiply(chunk):
+            for name, words, scales, bias, out, pooled in convs:
+                for i in range(chunk * CHUNK, (chunk + 1) * CHUNK):
+                    nc.tensor.matmul_mx(
+                        out=acc[name][:],
+                        lhsT=w_words[name, chunk][:, i % CHUNK, :].bitcast(FP8X4),
+                        lhsT_scale=w_scales[name][:, i, :],
+                        rhs=x_words[i][:].bitcast(FP8X4),
+                        rhs_scale=x_scales[i][:],
+                        start=(i == 0),
+                        stop=(i == PASSES - 1),
+                    )
+
+        for chunk in range(LEAD):
+            load_x(chunk)
+        for step in range(PASSES + QUANTISE_LAG):
+            if step < PASSES:
+                if step % CHUNK == 0:
+                    if step // CHUNK + LEAD < CHUNKS:
+                        load_x(step // CHUNK + LEAD)
+                    load_weights(step // CHUNK)
+                regroup(step)
+            if step >= QUANTISE_LAG:
+                quantise(step - QUANTISE_LAG)
+                if (step - QUANTISE_LAG) % CHUNK == CHUNK - 1:
+                    multiply((step - QUANTISE_LAG) // CHUNK)
+
+        for j, (name, words, scales, bias, out, pooled) in enumerate(convs):
+            biased = result_pool.tile([P, POSITIONS], F32, name="biased")
+            nc.scalar.activation(
+                out=biased[:],
+                in_=acc[name][:],
+                func=mybir.ActivationFunctionType.Identity,
+                bias=bias_f32[:, j : j + 1],
+            )
+            if pooled:
+                by_width = biased[:].rearrange("p (m b) -> p m b", b=2)
+                half = result_pool.tile([P, POSITIONS // 2], F32, name="half")
+                nc.vector.tensor_max(out=half[:], in0=by_width[:, :, 0], in1=by_width[:, :, 1])
+                by_height = half[:].rearrange("p (s a w) -> p s a w", a=2, w=4)
+                quarter = result_pool.tile([P, POSITIONS // 16, 4], F32, name="quarter")
+                nc.vector.tensor_max(
+                    out=quarter[:], in0=by_height[:, :, 0, :], in1=by_height[:, :, 1, :]
+                )
+                nc.sync.dma_start(out=out[0], in_=quarter[:].rearrange("p s w -> p (s w)"))
+            else:
+                nc.sync.dma_start(out=out[0], in_=biased[:])

@@ -63,30 +63,16 @@ def tile_nonlocalblocknd_pa_k_kernel(
         psum = ctx.enter_context(tc.psum_pool(name="psum", bufs=1))
         ctx.enter_context(tc.manual_schedule())
 
+        w_scales = keep.tile([P, PASSES, OUT_CHANNELS], U8, align_bytes=64)
+        nc.vector.memset(w_scales[:].bitcast(I32), 0)
+        for j, (name, words, scales, bias, out, pooled) in enumerate(convs):
+            rows = scales.bitcast(I32).rearrange("i (q r) n -> r q i n", r=4)
+            for r in range(4):
+                nc.sync.dma_start(out=w_scales[4 * j + r : P : 32].bitcast(I32), in_=rows[r])
+
         bias_bf16 = keep.tile([P, len(convs), 16], BF16)
         for j, (name, words, scales, bias, out, pooled) in enumerate(convs):
             nc.scalar.dma_start(out=bias_bf16[:, j, 0:1], in_=bias.rearrange("(p o) -> p o", o=1))
-        bias_f32 = keep.tile([P, len(convs)], F32)
-        nc.scalar.activation(
-            out=bias_f32[:],
-            in_=bias_bf16[:, :, 0],
-            func=mybir.ActivationFunctionType.Identity,
-        )
-
-        w_scales = {}
-        for name, words, scales, bias, out, pooled in convs:
-            w_scales[name] = keep.tile(
-                [P, PASSES, OUT_CHANNELS], U8, name="w_scales_" + name, align_bytes=64
-            )
-            nc.vector.memset(w_scales[name][:].bitcast(I32), 0)
-        for name, words, scales, bias, out, pooled in convs:
-            for quadrant in range(4):
-                nc.gpsimd.dma_start(
-                    out=w_scales[name][32 * quadrant : 32 * quadrant + 4].bitcast(F32),
-                    in_=scales.bitcast(F32)[:, 4 * quadrant : 4 * quadrant + 4, :].rearrange(
-                        "i r n -> r i n"
-                    ),
-                )
 
         acc = {}
         for name, words, scales, bias, out, pooled in convs:
@@ -133,12 +119,12 @@ def tile_nonlocalblocknd_pa_k_kernel(
             )
 
         def multiply(chunk):
-            for name, words, scales, bias, out, pooled in convs:
+            for j, (name, words, scales, bias, out, pooled) in enumerate(convs):
                 for i in range(chunk * CHUNK, (chunk + 1) * CHUNK):
                     nc.tensor.matmul_mx(
                         out=acc[name][:],
                         lhsT=w_words[name, chunk][:, i % CHUNK, :].bitcast(FP8X4),
-                        lhsT_scale=w_scales[name][:, i, :],
+                        lhsT_scale=w_scales[4 * j : P, i, :],
                         rhs=x_words[i][:].bitcast(FP8X4),
                         rhs_scale=x_scales[i][:],
                         start=(i == 0),
@@ -159,6 +145,12 @@ def tile_nonlocalblocknd_pa_k_kernel(
                 if (step - QUANTISE_LAG) % CHUNK == CHUNK - 1:
                     multiply((step - QUANTISE_LAG) // CHUNK)
 
+        bias_f32 = keep.tile([P, len(convs)], F32)
+        nc.scalar.activation(
+            out=bias_f32[:],
+            in_=bias_bf16[:, :, 0],
+            func=mybir.ActivationFunctionType.Identity,
+        )
         for j, (name, words, scales, bias, out, pooled) in enumerate(convs):
             biased = result_pool.tile([P, POSITIONS], F32, name="biased")
             nc.scalar.activation(

@@ -21,6 +21,7 @@ LEAD = 2
 QUANTISE_LAG = 2
 RAW_CHUNKS = 6
 QUANTISED_PASSES = 16
+DMA_ALIGN = 256
 
 FLOPS = 2 * 3 * OUT_CHANNELS * CHANNELS * POSITIONS
 
@@ -86,14 +87,16 @@ def tile_nonlocalblocknd_pa_k_kernel(
 
         def load_x(chunk):
             passes = slice(chunk * CHUNK, (chunk + 1) * CHUNK)
-            raw[chunk] = raw_pool.tile([P, CHUNK, PACK * POSITIONS], BF16, name="raw")
+            raw[chunk] = raw_pool.tile(
+                [P, CHUNK, PACK * POSITIONS], BF16, name="raw", align_bytes=DMA_ALIGN
+            )
             nc.sync.dma_start(out=raw[chunk][:], in_=x_by_pass[:, passes, :])
 
         def load_weights(chunk):
             passes = slice(chunk * CHUNK, (chunk + 1) * CHUNK)
             for name, words, scales, bias, out, pooled in convs:
                 w_words[name, chunk] = words_pool.tile(
-                    [P, CHUNK, OUT_CHANNELS], U32, name="w_words_" + name, align_bytes=64
+                    [P, CHUNK, OUT_CHANNELS], U32, name="w_words_" + name, align_bytes=DMA_ALIGN
                 )
                 nc.sync.dma_start(
                     out=w_words[name, chunk][:].bitcast(I32),

@@ -15,11 +15,12 @@ CHANNELS = 16384
 PASSES = CHANNELS // (P * PACK)
 POSITIONS = 8 * 8 * 8
 OUT_CHANNELS = 128
+X_PASSES = 2
 CHUNK = 4
 CHUNKS = PASSES // CHUNK
-LEAD = 2
+LEAD = 6
 QUANTISE_LAG = 2
-RAW_CHUNKS = 6
+RAW_TILES = 12
 QUANTISED_PASSES = 16
 DMA_ALIGN = 256
 
@@ -56,7 +57,7 @@ def tile_nonlocalblocknd_pa_k_kernel(
 
     with ExitStack() as ctx:
         keep = ctx.enter_context(tc.tile_pool(name="keep", bufs=1))
-        raw_pool = ctx.enter_context(tc.tile_pool(name="raw", bufs=RAW_CHUNKS))
+        raw_pool = ctx.enter_context(tc.tile_pool(name="raw", bufs=RAW_TILES))
         words_pool = ctx.enter_context(tc.tile_pool(name="words", bufs=CHUNKS))
         grouped_pool = ctx.enter_context(tc.tile_pool(name="grouped", bufs=QUANTISE_LAG + 2))
         quantised_pool = ctx.enter_context(tc.tile_pool(name="quantised", bufs=QUANTISED_PASSES))
@@ -64,7 +65,7 @@ def tile_nonlocalblocknd_pa_k_kernel(
         psum = ctx.enter_context(tc.psum_pool(name="psum", bufs=1))
         ctx.enter_context(tc.manual_schedule())
 
-        w_scales = keep.tile([P, PASSES, OUT_CHANNELS], U8, align_bytes=64)
+        w_scales = keep.tile([P, PASSES, OUT_CHANNELS], U8, align_bytes=DMA_ALIGN)
         nc.vector.memset(w_scales[:].bitcast(I32), 0)
         for j, (name, words, scales, bias, out, pooled) in enumerate(convs):
             rows = scales.bitcast(I32).rearrange("i (q r) n -> r q i n", r=4)
@@ -85,12 +86,13 @@ def tile_nonlocalblocknd_pa_k_kernel(
         x_words = {}
         x_scales = {}
 
-        def load_x(chunk):
-            passes = slice(chunk * CHUNK, (chunk + 1) * CHUNK)
-            raw[chunk] = raw_pool.tile(
-                [P, CHUNK, PACK * POSITIONS], BF16, name="raw", align_bytes=DMA_ALIGN
+        def load_x(first):
+            raw[first // X_PASSES] = raw_pool.tile(
+                [P, X_PASSES, PACK * POSITIONS], BF16, name="raw", align_bytes=DMA_ALIGN
             )
-            nc.sync.dma_start(out=raw[chunk][:], in_=x_by_pass[:, passes, :])
+            nc.sync.dma_start(
+                out=raw[first // X_PASSES][:], in_=x_by_pass[:, first : first + X_PASSES, :]
+            )
 
         def load_weights(chunk):
             passes = slice(chunk * CHUNK, (chunk + 1) * CHUNK)
@@ -107,7 +109,9 @@ def tile_nonlocalblocknd_pa_k_kernel(
 
         def regroup(i):
             grouped[i] = grouped_pool.tile([P, POSITIONS * PACK], BF16, name="grouped", align_bytes=64)
-            source = raw[i // CHUNK][:, i % CHUNK, :].rearrange("p (t c r) -> p c t r", t=PACK, r=4)
+            source = raw[i // X_PASSES][:, i % X_PASSES, :].rearrange(
+                "p (t c r) -> p c t r", t=PACK, r=4
+            )
             target = grouped[i][:].rearrange("p (c r t) -> p c t r", t=PACK, r=4)
             if i % 2 == 0:
                 nc.vector.tensor_copy(out=target, in_=source)
@@ -134,13 +138,13 @@ def tile_nonlocalblocknd_pa_k_kernel(
                         stop=(i == PASSES - 1),
                     )
 
-        for chunk in range(LEAD):
-            load_x(chunk)
+        for first in range(0, LEAD, X_PASSES):
+            load_x(first)
         for step in range(PASSES + QUANTISE_LAG):
             if step < PASSES:
+                if step % X_PASSES == 0 and step + LEAD < PASSES:
+                    load_x(step + LEAD)
                 if step % CHUNK == 0:
-                    if step // CHUNK + LEAD < CHUNKS:
-                        load_x(step // CHUNK + LEAD)
                     load_weights(step // CHUNK)
                 regroup(step)
             if step >= QUANTISE_LAG:
@@ -155,7 +159,7 @@ def tile_nonlocalblocknd_pa_k_kernel(
             func=mybir.ActivationFunctionType.Identity,
         )
         for j, (name, words, scales, bias, out, pooled) in enumerate(convs):
-            biased = result_pool.tile([P, POSITIONS], F32, name="biased")
+            biased = result_pool.tile([P, POSITIONS], F32, name="biased", align_bytes=DMA_ALIGN)
             nc.scalar.activation(
                 out=biased[:],
                 in_=acc[name][:],
@@ -167,7 +171,9 @@ def tile_nonlocalblocknd_pa_k_kernel(
                 half = result_pool.tile([P, POSITIONS // 2], F32, name="half")
                 nc.vector.tensor_max(out=half[:], in0=by_width[:, :, 0], in1=by_width[:, :, 1])
                 by_height = half[:].rearrange("p (s a w) -> p s a w", a=2, w=4)
-                quarter = result_pool.tile([P, POSITIONS // 16, 4], F32, name="quarter")
+                quarter = result_pool.tile(
+                    [P, POSITIONS // 16, 4], F32, name="quarter", align_bytes=DMA_ALIGN
+                )
                 nc.vector.tensor_max(
                     out=quarter[:], in0=by_height[:, :, 0, :], in1=by_height[:, :, 1, :]
                 )

@@ -8,6 +8,7 @@ I32 = mybir.dt.int32
 U32 = mybir.dt.uint32
 U8 = mybir.dt.uint8
 FP8X4 = mybir.dt.float8_e4m3fn_x4
+IDENTITY = mybir.ActivationFunctionType.Identity
 
 P = 128
 PACK = 4
@@ -16,13 +17,13 @@ PASSES = CHANNELS // (P * PACK)
 POSITIONS = 8 * 8 * 8
 OUT_CHANNELS = 128
 X_PASSES = 2
-CHUNK = 4
-CHUNKS = PASSES // CHUNK
+W_PASSES = 4
 LEAD = 6
 QUANTISE_LAG = 2
 RAW_TILES = 12
 QUANTISED_PASSES = 16
 DMA_ALIGN = 256
+MX_ALIGN = 64
 
 FLOPS = 2 * 3 * OUT_CHANNELS * CHANNELS * POSITIONS
 
@@ -45,11 +46,12 @@ def tile_nonlocalblocknd_pa_k_kernel(
 ):
     nc = tc.nc
 
-    convs = (
-        ("g", g_w_words, g_w_scales, g_b, out_0, True),
-        ("phi", phi_w_words, phi_w_scales, phi_b, out_2, True),
-        ("theta", theta_w_words, theta_w_scales, theta_b, out_1, False),
-    )
+    convs = ("g", "phi", "theta")
+    pooled = ("g", "phi")
+    words_in = {"g": g_w_words, "phi": phi_w_words, "theta": theta_w_words}
+    scales_in = {"g": g_w_scales, "phi": phi_w_scales, "theta": theta_w_scales}
+    bias_in = {"g": g_b, "phi": phi_b, "theta": theta_b}
+    result_out = {"g": out_0, "phi": out_2, "theta": out_1}
 
     x_by_pass = x.rearrange("b c f h w -> (b c) (f h w)").rearrange(
         "(i p t) n -> p i (t n)", p=P, t=PACK
@@ -58,33 +60,21 @@ def tile_nonlocalblocknd_pa_k_kernel(
     with ExitStack() as ctx:
         keep = ctx.enter_context(tc.tile_pool(name="keep", bufs=1))
         raw_pool = ctx.enter_context(tc.tile_pool(name="raw", bufs=RAW_TILES))
-        words_pool = ctx.enter_context(tc.tile_pool(name="words", bufs=CHUNKS))
+        words_pool = ctx.enter_context(tc.tile_pool(name="words", bufs=PASSES // W_PASSES))
         grouped_pool = ctx.enter_context(tc.tile_pool(name="grouped", bufs=QUANTISE_LAG + 2))
         quantised_pool = ctx.enter_context(tc.tile_pool(name="quantised", bufs=QUANTISED_PASSES))
         result_pool = ctx.enter_context(tc.tile_pool(name="result", bufs=2))
         psum = ctx.enter_context(tc.psum_pool(name="psum", bufs=1))
         ctx.enter_context(tc.manual_schedule())
 
-        w_scales = keep.tile([P, PASSES, OUT_CHANNELS], U8, align_bytes=DMA_ALIGN)
-        nc.vector.memset(w_scales[:].bitcast(I32), 0)
-        for j, (name, words, scales, bias, out, pooled) in enumerate(convs):
-            rows = scales.bitcast(I32).rearrange("i (q r) n -> r q i n", r=4)
-            for r in range(4):
-                nc.sync.dma_start(out=w_scales[4 * j + r : P : 32].bitcast(I32), in_=rows[r])
-
-        bias_bf16 = keep.tile([P, len(convs), 16], BF16)
-        for j, (name, words, scales, bias, out, pooled) in enumerate(convs):
-            nc.scalar.dma_start(out=bias_bf16[:, j, 0:1], in_=bias.rearrange("(p o) -> p o", o=1))
-
-        acc = {}
-        for name, words, scales, bias, out, pooled in convs:
-            acc[name] = psum.tile([P, POSITIONS], F32, name="acc_" + name)
-
         raw = {}
         w_words = {}
         grouped = {}
         x_words = {}
         x_scales = {}
+        acc = {}
+        for conv in convs:
+            acc[conv] = psum.tile([P, POSITIONS], F32, name="acc_" + conv)
 
         def load_x(first):
             raw[first // X_PASSES] = raw_pool.tile(
@@ -94,21 +84,23 @@ def tile_nonlocalblocknd_pa_k_kernel(
                 out=raw[first // X_PASSES][:], in_=x_by_pass[:, first : first + X_PASSES, :]
             )
 
-        def load_weights(chunk):
-            passes = slice(chunk * CHUNK, (chunk + 1) * CHUNK)
-            for name, words, scales, bias, out, pooled in convs:
-                w_words[name, chunk] = words_pool.tile(
-                    [P, CHUNK, OUT_CHANNELS], U32, name="w_words_" + name, align_bytes=DMA_ALIGN
+        def load_weights(first):
+            for conv in convs:
+                w_words[conv, first // W_PASSES] = words_pool.tile(
+                    [P, W_PASSES, OUT_CHANNELS], U32, name="w_words_" + conv, align_bytes=DMA_ALIGN
                 )
                 nc.sync.dma_start(
-                    out=w_words[name, chunk][:].bitcast(I32),
-                    in_=words.rearrange("i p n t -> i p (n t)")
+                    out=w_words[conv, first // W_PASSES][:].bitcast(I32),
+                    in_=words_in[conv]
+                    .rearrange("i p n t -> i p (n t)")
                     .bitcast(I32)
-                    .rearrange("i p n -> p i n")[:, passes, :],
+                    .rearrange("i p n -> p i n")[:, first : first + W_PASSES, :],
                 )
 
         def regroup(i):
-            grouped[i] = grouped_pool.tile([P, POSITIONS * PACK], BF16, name="grouped", align_bytes=64)
+            grouped[i] = grouped_pool.tile(
+                [P, POSITIONS * PACK], BF16, name="grouped", align_bytes=MX_ALIGN
+            )
             source = raw[i // X_PASSES][:, i % X_PASSES, :].rearrange(
                 "p (t c r) -> p c t r", t=PACK, r=4
             )
@@ -119,18 +111,22 @@ def tile_nonlocalblocknd_pa_k_kernel(
                 nc.scalar.copy(out=target, in_=source)
 
         def quantise(i):
-            x_words[i] = quantised_pool.tile([P, POSITIONS], U32, name="x_words", align_bytes=64)
-            x_scales[i] = quantised_pool.tile([P, POSITIONS], U8, name="x_scales", align_bytes=64)
+            x_words[i] = quantised_pool.tile(
+                [P, POSITIONS], U32, name="x_words", align_bytes=MX_ALIGN
+            )
+            x_scales[i] = quantised_pool.tile(
+                [P, POSITIONS], U8, name="x_scales", align_bytes=MX_ALIGN
+            )
             nc.vector.quantize_mx(
                 out=x_words[i][:].bitcast(FP8X4), scales=x_scales[i][:], in_=grouped[i][:]
             )
 
-        def multiply(chunk):
-            for j, (name, words, scales, bias, out, pooled) in enumerate(convs):
-                for i in range(chunk * CHUNK, (chunk + 1) * CHUNK):
+        def multiply(first):
+            for j, conv in enumerate(convs):
+                for i in range(first, first + W_PASSES):
                     nc.tensor.matmul_mx(
-                        out=acc[name][:],
-                        lhsT=w_words[name, chunk][:, i % CHUNK, :].bitcast(FP8X4),
+                        out=acc[conv][:],
+                        lhsT=w_words[conv, first // W_PASSES][:, i % W_PASSES, :].bitcast(FP8X4),
                         lhsT_scale=w_scales[4 * j : P, i, :],
                         rhs=x_words[i][:].bitcast(FP8X4),
                         rhs_scale=x_scales[i][:],
@@ -138,35 +134,42 @@ def tile_nonlocalblocknd_pa_k_kernel(
                         stop=(i == PASSES - 1),
                     )
 
-        for first in range(0, LEAD, X_PASSES):
+        w_scales = keep.tile([P, PASSES, OUT_CHANNELS], U8, align_bytes=DMA_ALIGN)
+        nc.vector.memset(w_scales[:].bitcast(I32), 0)
+        load_x(0)
+        for j, conv in enumerate(convs):
+            rows = scales_in[conv].bitcast(I32).rearrange("i (q r) n -> r q i n", r=4)
+            for r in range(4):
+                nc.sync.dma_start(out=w_scales[4 * j + r : P : 32].bitcast(I32), in_=rows[r])
+
+        bias_bf16 = keep.tile([P, len(convs), 16], BF16)
+        for j, conv in enumerate(convs):
+            nc.scalar.dma_start(
+                out=bias_bf16[:, j, 0:1], in_=bias_in[conv].rearrange("(p o) -> p o", o=1)
+            )
+
+        for first in range(X_PASSES, LEAD, X_PASSES):
             load_x(first)
         for step in range(PASSES + QUANTISE_LAG):
             if step < PASSES:
                 if step % X_PASSES == 0 and step + LEAD < PASSES:
                     load_x(step + LEAD)
-                if step % CHUNK == 0:
-                    load_weights(step // CHUNK)
+                if step % W_PASSES == 0:
+                    load_weights(step)
                 regroup(step)
             if step >= QUANTISE_LAG:
                 quantise(step - QUANTISE_LAG)
-                if (step - QUANTISE_LAG) % CHUNK == CHUNK - 1:
-                    multiply((step - QUANTISE_LAG) // CHUNK)
+                if (step - QUANTISE_LAG) % W_PASSES == W_PASSES - 1:
+                    multiply(step - QUANTISE_LAG - (W_PASSES - 1))
 
         bias_f32 = keep.tile([P, len(convs)], F32)
-        nc.scalar.activation(
-            out=bias_f32[:],
-            in_=bias_bf16[:, :, 0],
-            func=mybir.ActivationFunctionType.Identity,
-        )
-        for j, (name, words, scales, bias, out, pooled) in enumerate(convs):
+        nc.scalar.activation(out=bias_f32[:], in_=bias_bf16[:, :, 0], func=IDENTITY)
+        for j, conv in enumerate(convs):
             biased = result_pool.tile([P, POSITIONS], F32, name="biased", align_bytes=DMA_ALIGN)
             nc.scalar.activation(
-                out=biased[:],
-                in_=acc[name][:],
-                func=mybir.ActivationFunctionType.Identity,
-                bias=bias_f32[:, j : j + 1],
+                out=biased[:], in_=acc[conv][:], func=IDENTITY, bias=bias_f32[:, j : j + 1]
             )
-            if pooled:
+            if conv in pooled:
                 by_width = biased[:].rearrange("p (m b) -> p m b", b=2)
                 half = result_pool.tile([P, POSITIONS // 2], F32, name="half")
                 nc.vector.tensor_max(out=half[:], in0=by_width[:, :, 0], in1=by_width[:, :, 1])
@@ -177,6 +180,8 @@ def tile_nonlocalblocknd_pa_k_kernel(
                 nc.vector.tensor_max(
                     out=quarter[:], in0=by_height[:, :, 0, :], in1=by_height[:, :, 1, :]
                 )
-                nc.sync.dma_start(out=out[0], in_=quarter[:].rearrange("p s w -> p (s w)"))
+                nc.sync.dma_start(
+                    out=result_out[conv][0], in_=quarter[:].rearrange("p s w -> p (s w)")
+                )
             else:
-                nc.sync.dma_start(out=out[0], in_=biased[:])
+                nc.sync.dma_start(out=result_out[conv][0], in_=biased[:])

@@ -9,6 +9,8 @@ U32 = mybir.dt.uint32
 U8 = mybir.dt.uint8
 FP8X4 = mybir.dt.float8_e4m3fn_x4
 IDENTITY = mybir.ActivationFunctionType.Identity
+ADD = mybir.AluOpType.add
+MAX = mybir.AluOpType.max
 
 P = 128
 PACK = 4
@@ -18,10 +20,9 @@ POSITIONS = 8 * 8 * 8
 OUT_CHANNELS = 128
 X_PASSES = 2
 W_PASSES = 4
-LEAD = 6
-QUANTISE_LAG = 2
-RAW_TILES = 12
-QUANTISED_PASSES = 16
+LEAD = 4
+GROUPED_TILES = 4
+QUANTISED_PASSES = 10
 DMA_ALIGN = 256
 MX_ALIGN = 64
 
@@ -47,7 +48,6 @@ def tile_nonlocalblocknd_pa_k_kernel(
     nc = tc.nc
 
     convs = ("g", "phi", "theta")
-    pooled = ("g", "phi")
     words_in = {"g": g_w_words, "phi": phi_w_words, "theta": theta_w_words}
     scales_in = {"g": g_w_scales, "phi": phi_w_scales, "theta": theta_w_scales}
     bias_in = {"g": g_b, "phi": phi_b, "theta": theta_b}
@@ -59,9 +59,9 @@ def tile_nonlocalblocknd_pa_k_kernel(
 
     with ExitStack() as ctx:
         keep = ctx.enter_context(tc.tile_pool(name="keep", bufs=1))
-        raw_pool = ctx.enter_context(tc.tile_pool(name="raw", bufs=RAW_TILES))
+        raw_pool = ctx.enter_context(tc.tile_pool(name="raw", bufs=PASSES // X_PASSES))
         words_pool = ctx.enter_context(tc.tile_pool(name="words", bufs=PASSES // W_PASSES))
-        grouped_pool = ctx.enter_context(tc.tile_pool(name="grouped", bufs=QUANTISE_LAG + 2))
+        grouped_pool = ctx.enter_context(tc.tile_pool(name="grouped", bufs=GROUPED_TILES))
         quantised_pool = ctx.enter_context(tc.tile_pool(name="quantised", bufs=QUANTISED_PASSES))
         result_pool = ctx.enter_context(tc.tile_pool(name="result", bufs=2))
         psum = ctx.enter_context(tc.psum_pool(name="psum", bufs=1))
@@ -121,18 +121,17 @@ def tile_nonlocalblocknd_pa_k_kernel(
                 out=x_words[i][:].bitcast(FP8X4), scales=x_scales[i][:], in_=grouped[i][:]
             )
 
-        def multiply(first):
+        def multiply(i):
             for j, conv in enumerate(convs):
-                for i in range(first, first + W_PASSES):
-                    nc.tensor.matmul_mx(
-                        out=acc[conv][:],
-                        lhsT=w_words[conv, first // W_PASSES][:, i % W_PASSES, :].bitcast(FP8X4),
-                        lhsT_scale=w_scales[4 * j : P, i, :],
-                        rhs=x_words[i][:].bitcast(FP8X4),
-                        rhs_scale=x_scales[i][:],
-                        start=(i == 0),
-                        stop=(i == PASSES - 1),
-                    )
+                nc.tensor.matmul_mx(
+                    out=acc[conv][:],
+                    lhsT=w_words[conv, i // W_PASSES][:, i % W_PASSES, :].bitcast(FP8X4),
+                    lhsT_scale=w_scales[4 * j : P, i, :],
+                    rhs=x_words[i][:].bitcast(FP8X4),
+                    rhs_scale=x_scales[i][:],
+                    start=(i == 0),
+                    stop=(i == PASSES - 1),
+                )
 
         w_scales = keep.tile([P, PASSES, OUT_CHANNELS], U8, align_bytes=DMA_ALIGN)
         nc.vector.memset(w_scales[:].bitcast(I32), 0)
@@ -141,47 +140,54 @@ def tile_nonlocalblocknd_pa_k_kernel(
             rows = scales_in[conv].bitcast(I32).rearrange("i (q r) n -> r q i n", r=4)
             for r in range(4):
                 nc.sync.dma_start(out=w_scales[4 * j + r : P : 32].bitcast(I32), in_=rows[r])
-
-        bias_bf16 = keep.tile([P, len(convs), 16], BF16)
+        bias = keep.tile([P, len(convs), 16], BF16)
         for j, conv in enumerate(convs):
             nc.scalar.dma_start(
-                out=bias_bf16[:, j, 0:1], in_=bias_in[conv].rearrange("(p o) -> p o", o=1)
+                out=bias[:, j, 0:1], in_=bias_in[conv].rearrange("(p o) -> p o", o=1)
             )
+        for first in range(X_PASSES, PASSES - W_PASSES + LEAD, X_PASSES):
+            if first < PASSES:
+                load_x(first)
+            chunk = first + X_PASSES - LEAD
+            if chunk >= 0 and chunk % W_PASSES == 0:
+                load_weights(chunk)
 
-        for first in range(X_PASSES, LEAD, X_PASSES):
-            load_x(first)
-        for step in range(PASSES + QUANTISE_LAG):
-            if step < PASSES:
-                if step % X_PASSES == 0 and step + LEAD < PASSES:
-                    load_x(step + LEAD)
-                if step % W_PASSES == 0:
-                    load_weights(step)
-                regroup(step)
-            if step >= QUANTISE_LAG:
-                quantise(step - QUANTISE_LAG)
-                if (step - QUANTISE_LAG) % W_PASSES == W_PASSES - 1:
-                    multiply(step - QUANTISE_LAG - (W_PASSES - 1))
+        for even in range(0, PASSES, 2):
+            regroup(even)
+            regroup(even + 1)
+            if even > 0:
+                quantise(even - 1)
+                multiply(even - 1)
+            quantise(even)
+            multiply(even)
+        quantise(PASSES - 1)
+        multiply(PASSES - 1)
 
-        bias_f32 = keep.tile([P, len(convs)], F32)
-        nc.scalar.activation(out=bias_f32[:], in_=bias_bf16[:, :, 0], func=IDENTITY)
-        for j, conv in enumerate(convs):
-            biased = result_pool.tile([P, POSITIONS], F32, name="biased", align_bytes=DMA_ALIGN)
+        pooled = ("g", "phi")
+        low = keep.tile([P, len(pooled), POSITIONS // 16, 8], F32)
+        tall = keep.tile([P, len(pooled), POSITIONS // 16, 8], F32)
+        quarter = keep.tile([P, len(pooled), POSITIONS // 4], F32, align_bytes=DMA_ALIGN)
+        biased = keep.tile([P, POSITIONS], F32, align_bytes=DMA_ALIGN)
+        for j, conv in enumerate(pooled):
             nc.scalar.activation(
-                out=biased[:], in_=acc[conv][:], func=IDENTITY, bias=bias_f32[:, j : j + 1]
+                out=low[:, j],
+                in_=acc[conv][:].rearrange("p (s a w) -> p s a w", a=2, w=8)[:, :, 1, :],
+                func=IDENTITY,
+                bias=bias[:, j, 0:1],
             )
-            if conv in pooled:
-                by_width = biased[:].rearrange("p (m b) -> p m b", b=2)
-                half = result_pool.tile([P, POSITIONS // 2], F32, name="half")
-                nc.vector.tensor_max(out=half[:], in0=by_width[:, :, 0], in1=by_width[:, :, 1])
-                by_height = half[:].rearrange("p (s a w) -> p s a w", a=2, w=4)
-                quarter = result_pool.tile(
-                    [P, POSITIONS // 16, 4], F32, name="quarter", align_bytes=DMA_ALIGN
-                )
-                nc.vector.tensor_max(
-                    out=quarter[:], in0=by_height[:, :, 0, :], in1=by_height[:, :, 1, :]
-                )
-                nc.sync.dma_start(
-                    out=result_out[conv][0], in_=quarter[:].rearrange("p s w -> p (s w)")
-                )
-            else:
-                nc.sync.dma_start(out=result_out[conv][0], in_=biased[:])
+            nc.vector.scalar_tensor_tensor(
+                out=tall[:, j],
+                in0=acc[conv][:].rearrange("p (s a w) -> p s a w", a=2, w=8)[:, :, 0, :],
+                scalar=bias[:, j, 0:1],
+                in1=low[:, j],
+                op0=ADD,
+                op1=MAX,
+            )
+        nc.scalar.activation(out=biased[:], in_=acc["theta"][:], func=IDENTITY, bias=bias[:, 2, 0:1])
+        nc.scalar.dma_start(out=result_out["theta"][0], in_=biased[:])
+        by_width = tall[:].rearrange("p j s (w b) -> p (j s w) b", b=2)
+        nc.vector.tensor_max(
+            out=quarter[:].rearrange("p j m -> p (j m)"), in0=by_width[:, :, 0], in1=by_width[:, :, 1]
+        )
+        for j, conv in enumerate(pooled):
+            nc.sync.dma_start(out=result_out[conv][0], in_=quarter[:, j, :])

@@ -21,6 +21,7 @@ OUT_CHANNELS = 128
 X_PASSES = 2
 W_PASSES = 4
 LEAD = 4
+SCALE_RUN = 3
 GROUPED_TILES = 4
 QUANTISED_PASSES = 10
 DMA_ALIGN = 256
@@ -135,22 +136,31 @@ def tile_nonlocalblocknd_pa_k_kernel(
 
         w_scales = keep.tile([P, PASSES, OUT_CHANNELS], U8, align_bytes=DMA_ALIGN)
         nc.vector.memset(w_scales[:].bitcast(I32), 0)
-        load_x(0)
-        for j, conv in enumerate(convs):
-            rows = scales_in[conv].bitcast(I32).rearrange("i (q r) n -> r q i n", r=4)
-            for r in range(4):
-                nc.sync.dma_start(out=w_scales[4 * j + r : P : 32].bitcast(I32), in_=rows[r])
         bias = keep.tile([P, len(convs), 16], BF16)
         for j, conv in enumerate(convs):
             nc.scalar.dma_start(
                 out=bias[:, j, 0:1], in_=bias_in[conv].rearrange("(p o) -> p o", o=1)
             )
+
+        scale_loads = [(j, r) for r in range(4) for j in range(len(convs))]
+        scale_loads_issued = [0]
+
+        def load_scales(count):
+            for j, r in scale_loads[scale_loads_issued[0] : scale_loads_issued[0] + count]:
+                rows = scales_in[convs[j]].bitcast(I32).rearrange("i (q r) n -> r q i n", r=4)
+                nc.sync.dma_start(out=w_scales[4 * j + r : P : 32].bitcast(I32), in_=rows[r])
+            scale_loads_issued[0] += count
+
+        load_x(0)
+        load_scales(SCALE_RUN)
         for first in range(X_PASSES, PASSES - W_PASSES + LEAD, X_PASSES):
             if first < PASSES:
                 load_x(first)
+                load_scales(SCALE_RUN)
             chunk = first + X_PASSES - LEAD
             if chunk >= 0 and chunk % W_PASSES == 0:
                 load_weights(chunk)
+                load_scales(SCALE_RUN)
 
         for even in range(0, PASSES, 2):
             regroup(even)

@@ -18,8 +18,8 @@ CHANNELS = 16384
 PASSES = CHANNELS // (P * PACK)
 POSITIONS = 8 * 8 * 8
 OUT_CHANNELS = 128
-X_PASSES = 2
-W_PASSES = 4
+X_LOADS = (2, 2, 4, 4, 4, 4, 2, 2, 2, 2, 2, 2)
+W_LOADS = (4, 8, 8, 4, 4, 4)
 LEAD = 4
 SCALE_RUN = 3
 GROUPED_TILES = 4
@@ -60,8 +60,8 @@ def tile_nonlocalblocknd_pa_k_kernel(
 
     with ExitStack() as ctx:
         keep = ctx.enter_context(tc.tile_pool(name="keep", bufs=1))
-        raw_pool = ctx.enter_context(tc.tile_pool(name="raw", bufs=PASSES // X_PASSES))
-        words_pool = ctx.enter_context(tc.tile_pool(name="words", bufs=PASSES // W_PASSES))
+        raw_pool = ctx.enter_context(tc.tile_pool(name="raw", bufs=1))
+        words_pool = ctx.enter_context(tc.tile_pool(name="words", bufs=1))
         grouped_pool = ctx.enter_context(tc.tile_pool(name="grouped", bufs=GROUPED_TILES))
         quantised_pool = ctx.enter_context(tc.tile_pool(name="quantised", bufs=QUANTISED_PASSES))
         result_pool = ctx.enter_context(tc.tile_pool(name="result", bufs=2))
@@ -77,32 +77,41 @@ def tile_nonlocalblocknd_pa_k_kernel(
         for conv in convs:
             acc[conv] = psum.tile([P, POSITIONS], F32, name="acc_" + conv)
 
-        def load_x(first):
-            raw[first // X_PASSES] = raw_pool.tile(
-                [P, X_PASSES, PACK * POSITIONS], BF16, name="raw", align_bytes=DMA_ALIGN
+        def load_x(first, count):
+            loaded = raw_pool.tile(
+                [P, count, PACK * POSITIONS],
+                BF16,
+                name="raw%d" % count,
+                bufs=len([c for c in X_LOADS if c == count]),
+                align_bytes=DMA_ALIGN,
+            )
+            nc.sync.dma_start(out=loaded[:], in_=x_by_pass[:, first : first + count, :])
+            for i in range(count):
+                raw[first + i] = loaded[:, i, :]
+
+        def load_weights(conv, first, count):
+            loaded = words_pool.tile(
+                [P, count, OUT_CHANNELS],
+                U32,
+                name="w_words_%s%d" % (conv, count),
+                bufs=len([c for c in W_LOADS if c == count]),
+                align_bytes=DMA_ALIGN,
             )
             nc.sync.dma_start(
-                out=raw[first // X_PASSES][:], in_=x_by_pass[:, first : first + X_PASSES, :]
+                out=loaded[:].bitcast(I32),
+                in_=words_in[conv]
+                .rearrange("i p n t -> i p (n t)")
+                .bitcast(I32)
+                .rearrange("i p n -> p i n")[:, first : first + count, :],
             )
-
-        def load_weights(first):
-            for conv in convs:
-                w_words[conv, first // W_PASSES] = words_pool.tile(
-                    [P, W_PASSES, OUT_CHANNELS], U32, name="w_words_" + conv, align_bytes=DMA_ALIGN
-                )
-                nc.sync.dma_start(
-                    out=w_words[conv, first // W_PASSES][:].bitcast(I32),
-                    in_=words_in[conv]
-                    .rearrange("i p n t -> i p (n t)")
-                    .bitcast(I32)
-                    .rearrange("i p n -> p i n")[:, first : first + W_PASSES, :],
-                )
+            for i in range(count):
+                w_words[conv, first + i] = loaded[:, i, :]
 
         def regroup(i):
             grouped[i] = grouped_pool.tile(
                 [P, POSITIONS * PACK], BF16, name="grouped", align_bytes=MX_ALIGN
             )
-            source = raw[i // X_PASSES][:, i % X_PASSES, :].rearrange(
+            source = raw[i].rearrange(
                 "p (t c r) -> p c t r", t=PACK, r=4
             )
             target = grouped[i][:].rearrange("p (c r t) -> p c t r", t=PACK, r=4)
@@ -126,7 +135,7 @@ def tile_nonlocalblocknd_pa_k_kernel(
             for j, conv in enumerate(convs):
                 nc.tensor.matmul_mx(
                     out=acc[conv][:],
-                    lhsT=w_words[conv, i // W_PASSES][:, i % W_PASSES, :].bitcast(FP8X4),
+                    lhsT=w_words[conv, i].bitcast(FP8X4),
                     lhsT_scale=w_scales[4 * j : P, i, :],
                     rhs=x_words[i][:].bitcast(FP8X4),
                     rhs_scale=x_scales[i][:],
@@ -151,15 +160,23 @@ def tile_nonlocalblocknd_pa_k_kernel(
                 nc.sync.dma_start(out=w_scales[4 * j + r : P : 32].bitcast(I32), in_=rows[r])
             scale_loads_issued[0] += count
 
-        load_x(0)
-        load_scales(SCALE_RUN)
-        for first in range(X_PASSES, PASSES - W_PASSES + LEAD, X_PASSES):
-            if first < PASSES:
-                load_x(first)
-                load_scales(SCALE_RUN)
-            chunk = first + X_PASSES - LEAD
-            if chunk >= 0 and chunk % W_PASSES == 0:
-                load_weights(chunk)
+        loads = []
+        first = 0
+        for count in X_LOADS:
+            loads.append((float(first), 1, "x", first, count))
+            first += count
+        first = 0
+        for count in W_LOADS:
+            for j, conv in enumerate(convs):
+                place = first + LEAD - count + (j + 1) * count / 3.0
+                loads.append((max(place, 0.5), 0, conv, first, count))
+            first += count
+        for place, after, what, first, count in sorted(loads):
+            if what == "x":
+                load_x(first, count)
+            else:
+                load_weights(what, first, count)
+            if what == "x" or (what, first) == (convs[-1], 0):
                 load_scales(SCALE_RUN)
 
         for even in range(0, PASSES, 2):

@@ -145,11 +145,6 @@ def tile_nonlocalblocknd_pa_k_kernel(
 
         w_scales = keep.tile([P, PASSES, OUT_CHANNELS], U8, align_bytes=DMA_ALIGN)
         nc.vector.memset(w_scales[:].bitcast(I32), 0)
-        bias = keep.tile([P, len(convs), 16], BF16)
-        for j, conv in enumerate(convs):
-            nc.scalar.dma_start(
-                out=bias[:, j, 0:1], in_=bias_in[conv].rearrange("(p o) -> p o", o=1)
-            )
 
         scale_loads = [(j, r) for r in range(4) for j in range(len(convs))]
         scale_loads_issued = [0]
@@ -178,6 +173,11 @@ def tile_nonlocalblocknd_pa_k_kernel(
                 load_weights(what, first, count)
             if what == "x" or (what, first) == (convs[-1], 0):
                 load_scales(SCALE_RUN)
+        bias = keep.tile([P, len(convs), 16], BF16)
+        for j, conv in enumerate(convs):
+            nc.sync.dma_start(
+                out=bias[:, j, 0:1], in_=bias_in[conv].rearrange("(p o) -> p o", o=1)
+            )
 
         for even in range(0, PASSES, 2):
             regroup(even)

@@ -19,7 +19,7 @@ PASSES = CHANNELS // (P * PACK)
 POSITIONS = 8 * 8 * 8
 OUT_CHANNELS = 128
 X_LOADS = (2, 2, 4, 4, 4, 4, 2, 2, 2, 2, 2, 2)
-W_LOADS = (4, 8, 8, 4, 4, 4)
+W_LOADS = (4, 8, 8, 4, 4, 2, 2)
 LEAD = 4
 SCALE_RUN = 3
 GROUPED_TILES = 4
@@ -158,15 +158,14 @@ def tile_nonlocalblocknd_pa_k_kernel(
         loads = []
         first = 0
         for count in X_LOADS:
-            loads.append((float(first), 1, "x", first, count))
+            loads.append((float(first), 1, 0, "x", first, count))
             first += count
         first = 0
         for count in W_LOADS:
             for j, conv in enumerate(convs):
-                place = first + LEAD - count + (j + 1) * count / 3.0
-                loads.append((max(place, 0.5), 0, conv, first, count))
+                loads.append((first + LEAD - 0.5, 0, j, conv, first, count))
             first += count
-        for place, after, what, first, count in sorted(loads):
+        for place, after, j, what, first, count in sorted(loads):
             if what == "x":
                 load_x(first, count)
             else:

from contextlib import ExitStack

import concourse.mybir as mybir

BF16 = mybir.dt.bfloat16
F32 = mybir.dt.float32
I32 = mybir.dt.int32
U32 = mybir.dt.uint32
U8 = mybir.dt.uint8
FP8X4 = mybir.dt.float8_e4m3fn_x4
IDENTITY = mybir.ActivationFunctionType.Identity
ADD = mybir.AluOpType.add
MAX = mybir.AluOpType.max

P = 128
PACK = 4
CHANNELS = 16384
PASSES = CHANNELS // (P * PACK)
POSITIONS = 8 * 8 * 8
OUT_CHANNELS = 128
X_LOADS = (2, 2, 4, 4, 4, 4, 2, 2, 2, 2, 2, 2)
W_LOADS = (4, 8, 8, 4, 4, 2, 2)
LEAD = 4
SCALE_RUN = 3
GROUPED_TILES = 4
QUANTISED_PASSES = 10
DMA_ALIGN = 256
MX_ALIGN = 64

FLOPS = 2 * 3 * OUT_CHANNELS * CHANNELS * POSITIONS


def tile_nonlocalblocknd_pa_k_kernel(
    tc,
    x,
    g_w_words,
    g_w_scales,
    g_b,
    theta_w_words,
    theta_w_scales,
    theta_b,
    phi_w_words,
    phi_w_scales,
    phi_b,
    out_0,
    out_1,
    out_2,
):
    nc = tc.nc

    convs = ("g", "phi", "theta")
    words_in = {"g": g_w_words, "phi": phi_w_words, "theta": theta_w_words}
    scales_in = {"g": g_w_scales, "phi": phi_w_scales, "theta": theta_w_scales}
    bias_in = {"g": g_b, "phi": phi_b, "theta": theta_b}
    result_out = {"g": out_0, "phi": out_2, "theta": out_1}

    x_by_pass = x.rearrange("b c f h w -> (b c) (f h w)").rearrange(
        "(i p t) n -> p i (t n)", p=P, t=PACK
    )

    with ExitStack() as ctx:
        keep = ctx.enter_context(tc.tile_pool(name="keep", bufs=1))
        raw_pool = ctx.enter_context(tc.tile_pool(name="raw", bufs=1))
        words_pool = ctx.enter_context(tc.tile_pool(name="words", bufs=1))
        grouped_pool = ctx.enter_context(tc.tile_pool(name="grouped", bufs=GROUPED_TILES))
        quantised_pool = ctx.enter_context(tc.tile_pool(name="quantised", bufs=QUANTISED_PASSES))
        result_pool = ctx.enter_context(tc.tile_pool(name="result", bufs=2))
        psum = ctx.enter_context(tc.psum_pool(name="psum", bufs=1))
        ctx.enter_context(tc.manual_schedule())

        raw = {}
        w_words = {}
        grouped = {}
        x_words = {}
        x_scales = {}
        acc = {}
        for conv in convs:
            acc[conv] = psum.tile([P, POSITIONS], F32, name="acc_" + conv)

        def load_x(first, count):
            loaded = raw_pool.tile(
                [P, count, PACK * POSITIONS],
                BF16,
                name="raw%d" % count,
                bufs=len([c for c in X_LOADS if c == count]),
                align_bytes=DMA_ALIGN,
            )
            nc.sync.dma_start(out=loaded[:], in_=x_by_pass[:, first : first + count, :])
            for i in range(count):
                raw[first + i] = loaded[:, i, :]

        def load_weights(conv, first, count):
            loaded = words_pool.tile(
                [P, count, OUT_CHANNELS],
                U32,
                name="w_words_%s%d" % (conv, count),
                bufs=len([c for c in W_LOADS if c == count]),
                align_bytes=DMA_ALIGN,
            )
            nc.sync.dma_start(
                out=loaded[:].bitcast(I32),
                in_=words_in[conv]
                .rearrange("i p n t -> i p (n t)")
                .bitcast(I32)
                .rearrange("i p n -> p i n")[:, first : first + count, :],
            )
            for i in range(count):
                w_words[conv, first + i] = loaded[:, i, :]

        def regroup(i):
            grouped[i] = grouped_pool.tile(
                [P, POSITIONS * PACK], BF16, name="grouped", align_bytes=MX_ALIGN
            )
            source = raw[i].rearrange(
                "p (t c r) -> p c t r", t=PACK, r=4
            )
            target = grouped[i][:].rearrange("p (c r t) -> p c t r", t=PACK, r=4)
            if i % 2 == 0:
                nc.vector.tensor_copy(out=target, in_=source)
            else:
                nc.scalar.copy(out=target, in_=source)

        def quantise(i):
            x_words[i] = quantised_pool.tile(
                [P, POSITIONS], U32, name="x_words", align_bytes=MX_ALIGN
            )
            x_scales[i] = quantised_pool.tile(
                [P, POSITIONS], U8, name="x_scales", align_bytes=MX_ALIGN
            )
            nc.vector.quantize_mx(
                out=x_words[i][:].bitcast(FP8X4), scales=x_scales[i][:], in_=grouped[i][:]
            )

        def multiply(i):
            for j, conv in enumerate(convs):
                nc.tensor.matmul_mx(
                    out=acc[conv][:],
                    lhsT=w_words[conv, i].bitcast(FP8X4),
                    lhsT_scale=w_scales[4 * j : P, i, :],
                    rhs=x_words[i][:].bitcast(FP8X4),
                    rhs_scale=x_scales[i][:],
                    start=(i == 0),
                    stop=(i == PASSES - 1),
                )

        w_scales = keep.tile([P, PASSES, OUT_CHANNELS], U8, align_bytes=DMA_ALIGN)
        nc.vector.memset(w_scales[:].bitcast(I32), 0)

        scale_loads = [(j, r) for r in range(4) for j in range(len(convs))]
        scale_loads_issued = [0]

        def load_scales(count):
            for j, r in scale_loads[scale_loads_issued[0] : scale_loads_issued[0] + count]:
                rows = scales_in[convs[j]].bitcast(I32).rearrange("i (q r) n -> r q i n", r=4)
                nc.sync.dma_start(out=w_scales[4 * j + r : P : 32].bitcast(I32), in_=rows[r])
            scale_loads_issued[0] += count

        loads = []
        first = 0
        for count in X_LOADS:
            loads.append((float(first), 1, 0, "x", first, count))
            first += count
        first = 0
        for count in W_LOADS:
            for j, conv in enumerate(convs):
                loads.append((first + LEAD - 0.5, 0, j, conv, first, count))
            first += count
        for place, after, j, what, first, count in sorted(loads):
            if what == "x":
                load_x(first, count)
            else:
                load_weights(what, first, count)
            if what == "x" or (what, first) == (convs[-1], 0):
                load_scales(SCALE_RUN)
        bias = keep.tile([P, len(convs), 16], BF16)
        for j, conv in enumerate(convs):
            nc.sync.dma_start(
                out=bias[:, j, 0:1], in_=bias_in[conv].rearrange("(p o) -> p o", o=1)
            )

        for even in range(0, PASSES, 2):
            regroup(even)
            regroup(even + 1)
            if even > 0:
                quantise(even - 1)
                multiply(even - 1)
            quantise(even)
            multiply(even)
        quantise(PASSES - 1)
        multiply(PASSES - 1)

        pooled = ("g", "phi")
        low = keep.tile([P, len(pooled), POSITIONS // 16, 8], F32)
        tall = keep.tile([P, len(pooled), POSITIONS // 16, 8], F32)
        quarter = keep.tile([P, len(pooled), POSITIONS // 4], F32, align_bytes=DMA_ALIGN)
        biased = keep.tile([P, POSITIONS], F32, align_bytes=DMA_ALIGN)
        for j, conv in enumerate(pooled):
            nc.scalar.activation(
                out=low[:, j],
                in_=acc[conv][:].rearrange("p (s a w) -> p s a w", a=2, w=8)[:, :, 1, :],
                func=IDENTITY,
                bias=bias[:, j, 0:1],
            )
            nc.vector.scalar_tensor_tensor(
                out=tall[:, j],
                in0=acc[conv][:].rearrange("p (s a w) -> p s a w", a=2, w=8)[:, :, 0, :],
                scalar=bias[:, j, 0:1],
                in1=low[:, j],
                op0=ADD,
                op1=MAX,
            )
        nc.scalar.activation(out=biased[:], in_=acc["theta"][:], func=IDENTITY, bias=bias[:, 2, 0:1])
        nc.scalar.dma_start(out=result_out["theta"][0], in_=biased[:])
        by_width = tall[:].rearrange("p j s (w b) -> p (j s w) b", b=2)
        nc.vector.tensor_max(
            out=quarter[:].rearrange("p j m -> p (j m)"), in0=by_width[:, :, 0], in1=by_width[:, :, 1]
        )
        for j, conv in enumerate(pooled):
            nc.sync.dma_start(out=result_out[conv][0], in_=quarter[:, j, :])
